import numpy as np
import ml_dtypes


def mxq(x, axis, fmt="e4m3"):
    dtype, down = {"e4m3": (ml_dtypes.float8_e4m3fn, 7), "e5m2": (ml_dtypes.float8_e5m2, 14)}[fmt]
    v = np.moveaxis(np.asarray(x, np.float32).astype(ml_dtypes.bfloat16).astype(np.float64), axis, -1)
    blocks = v.reshape(v.shape[:-1] + (-1, 32))
    amax = np.abs(blocks).max(-1, keepdims=True)
    byte = np.maximum(np.where(amax > 0, np.frexp(amax)[1] - 1 + 127, 0) - down, 1)
    scale = np.exp2(byte - 127.0)
    codes = (blocks / scale).astype(np.float32).astype(dtype).astype(np.float64)
    return np.moveaxis((codes * scale).reshape(v.shape), -1, axis)


WIDE = False


def mx_kscale(k):
    if not WIDE:
        return np.ones(k)
    levels = np.array([10, -10, 5, -5, 0])
    a = np.random.permutation(np.resize(levels, k // 512 * 4)).reshape(k // 512, 4)
    idx = np.arange(k)
    return np.exp2(a[idx // 512, idx % 128 // 32])


BF16 = ml_dtypes.bfloat16


def bf(x):
    return np.asarray(x, np.float32).astype(BF16)


def f64(x):
    return np.asarray(x).astype(np.float64)


B, N, G, KT = 8, 1024, 128, 4


def tap_scale():
    t = mx_kscale(KT * G).reshape(KT, G).copy()
    t[KT - 1] = t[KT - 2]
    return t


def setup_inputs():
    ta, tb = tap_scale(), tap_scale()
    return {"x_taps": bf(np.random.standard_normal((B, KT - 1, G, N)) * ta[None, :KT - 1, :, None]),
            "h_taps": bf(np.random.standard_normal((B, KT - 1, G, N)) * tb[None, :KT - 1, :, None]),
            "S": bf(np.random.standard_normal((B, N, N)) / np.sqrt(N)),
            "weight_A": bf(np.random.standard_normal((G, KT, G)) / np.sqrt(KT * G) / ta[None]),
            "weight_B": bf(np.random.standard_normal((G, KT, G)) / np.sqrt(KT * G) / tb[None]),
            "bias_A": bf(np.random.standard_normal(G) * 0.3)[:, None],
            "bias_B": bf(np.random.standard_normal(G) * 0.3)[:, None]}


def filter_tail(taps, Sq, w, b):
    last = mxq(taps[:, KT - 2], 2, "e4m3") @ Sq
    z = np.concatenate([taps, last[:, None]], axis=1).reshape(B, KT * G, N)
    return (mxq(w.reshape(G, KT * G), 1, "e4m3") @ mxq(z, 1, "e4m3")) + b


def reference(x_taps, h_taps, S, weight_A, weight_B, bias_A, bias_B):
    Sq = mxq(f64(S), 1, "e4m3")
    u_a = filter_tail(f64(x_taps), Sq, f64(weight_A), f64(bias_A))
    u_b = filter_tail(f64(h_taps), Sq, f64(weight_B), f64(bias_B))
    return np.maximum(u_a + u_b, 0.0)

@@ -1,0 +1,309 @@
+from contextlib import ExitStack
+
+import concourse.mybir as mybir
+from concourse.masks import make_identity
+
+FP8X4 = mybir.dt.float8_e4m3fn_x4
+BF16 = mybir.dt.bfloat16
+F32 = mybir.dt.float32
+U32 = mybir.dt.uint32
+U8 = mybir.dt.uint8
+RELU = mybir.ActivationFunctionType.Relu
+
+B = 8
+N = 1024
+G = 128
+KT = 4
+P = 128
+HALF = 512
+
+FLOPS = B * 2 * (2 * G * N * N + 2 * G * KT * G * N)
+
+MANUAL = True
+V_COLS_S = [832, 960, 960, 1024, 1024, 1024, 1024, 1024]
+V_COLS_Z = [448, 320, 320, 320, 384, 320, 320, 832]
+
+
+def tile_graphfilterrnnbatch_pb_kernel(
+    tc, x_taps, h_taps, S, weight_A, weight_B, bias_A, bias_B, out
+):
+    nc = tc.nc
+    taps_in = [x_taps, h_taps]
+    with ExitStack() as ctx:
+        const = ctx.enter_context(tc.tile_pool(name="const", bufs=1))
+        sraw_pool = ctx.enter_context(tc.tile_pool(name="sraw", bufs=3))
+        sgrp_pool = ctx.enter_context(tc.tile_pool(name="sgrp", bufs=3))
+        scode_pool = ctx.enter_context(tc.tile_pool(name="scode", bufs=2))
+        taps_pool = ctx.enter_context(tc.tile_pool(name="taps", bufs=3))
+        zgrp_pool = ctx.enter_context(tc.tile_pool(name="zgrp", bufs=4))
+        zcode_pool = ctx.enter_context(tc.tile_pool(name="zcode", bufs=4))
+        xt_pool = ctx.enter_context(tc.tile_pool(name="xt", bufs=2))
+        out_pool = ctx.enter_context(tc.tile_pool(name="outp", bufs=3))
+        ps_t = ctx.enter_context(tc.psum_pool(name="ps_t", bufs=2))
+        ps_1 = ctx.enter_context(tc.psum_pool(name="ps_1", bufs=4))
+        ps_2 = ctx.enter_context(tc.psum_pool(name="ps_2", bufs=2))
+        if MANUAL:
+            ctx.enter_context(tc.manual_schedule())
+
+        s_raw = {}
+        s_codes = {}
+        s_scales = {}
+        taps = {}
+        xt_grp = {}
+        xt_codes = {}
+        xt_scales = {}
+        z_grp = {}
+        z_codes = {}
+        z_scales = {}
+        acc2 = {}
+
+        def load_s(g):
+            s_raw[g] = sraw_pool.tile([P, 2, 4, N], BF16, name="s_raw", tag="s_raw")
+            for c in range(2):
+                nc.sync.dma_start(
+                    out=s_raw[g][:, c],
+                    in_=S[g, c * 512 : (c + 1) * 512, :].rearrange("(p j) m -> p j m", j=4),
+                )
+
+        def load_taps(g):
+            for xh in range(2):
+                taps[(g, xh)] = taps_pool.tile(
+                    [P, KT, N], BF16, name="taps%d" % xh, tag="taps%d" % xh
+                )
+                nc.sync.dma_start(
+                    out=taps[(g, xh)][:, 0 : KT - 1, :],
+                    in_=taps_in[xh][g].rearrange("t f n -> f t n"),
+                )
+
+        def regroup(dst, src, lo, hi, engine_copy):
+            engine_copy(
+                out=dst[:, lo:hi, :].rearrange("p (c i) t -> p c t i", i=4),
+                in_=src[:, :, lo:hi].rearrange("p t (c i) -> p c t i", i=4),
+            )
+
+        s_grp = {}
+
+        def regroup_s(g, c):
+            s_grp[(g, c)] = sgrp_pool.tile(
+                [P, N, 4], BF16, name="s_grp", tag="s_grp", align_bytes=64
+            )
+            regroup(s_grp[(g, c)], s_raw[g][:, c], 0, V_COLS_S[g], nc.vector.tensor_copy)
+            if V_COLS_S[g] < N:
+                regroup(s_grp[(g, c)], s_raw[g][:, c], V_COLS_S[g], N, nc.scalar.copy)
+
+        def quant_s(g, c):
+            if c == 0:
+                s_codes[g] = scode_pool.tile(
+                    [P, 2, N], U32, name="s_codes", tag="s_codes", align_bytes=64
+                )
+                s_scales[g] = scode_pool.tile(
+                    [P, 2, N], U8, name="s_scales", tag="s_scales", align_bytes=64
+                )
+            nc.vector.quantize_mx(
+                out=s_codes[g][:, c, :].bitcast(FP8X4),
+                scales=s_scales[g][:, c, :],
+                in_=s_grp[(g, c)][:].rearrange("p m j -> p (m j)"),
+            )
+
+        def transpose_x2(g):
+            xt_grp[g] = xt_pool.tile([P, 4 * 512], BF16, name="xt_grp", tag="xt_grp", align_bytes=64)
+            dst = xt_grp[g][:].bitcast(F32).rearrange("p (x c f u) -> p x c f u", x=2, c=2, u=2)
+            for xh in range(2):
+                tp = ps_t.tile([P, 2, 2, P], F32, name="tp", tag="tp")
+                words = (
+                    taps[(g, xh)][:, KT - 2, :]
+                    .bitcast(F32)
+                    .rearrange("f (c p u) -> f c u p", c=2, u=2)
+                )
+                for c in range(2):
+                    for u in range(2):
+                        nc.tensor.transpose(tp[:, c, u, :], words[:, c, u, :], ident_f[:])
+                nc.scalar.copy(out=dst[:, xh], in_=tp[:].rearrange("p c u f -> p c f u"))
+
+        def quant_xt(g):
+            xt_codes[g] = xt_pool.tile([P, 512], U32, name="xt_codes", tag="xt_codes", align_bytes=64)
+            xt_scales[g] = xt_pool.tile([P, 512], U8, name="xt_scales", tag="xt_scales", align_bytes=64)
+            nc.vector.quantize_mx(
+                out=xt_codes[g][:].bitcast(FP8X4), scales=xt_scales[g][:], in_=xt_grp[g][:]
+            )
+
+        def shift(g, xh, mh):
+            cols = slice(mh * HALF, (mh + 1) * HALF)
+            acc = ps_1.tile([P, HALF], F32, name="acc1", tag="acc1")
+            for c in range(2):
+                w = slice((xh * 2 + c) * P, (xh * 2 + c + 1) * P)
+                nc.tensor.matmul_mx(
+                    out=acc[:],
+                    lhsT=xt_codes[g][:, w].bitcast(FP8X4),
+                    lhsT_scale=xt_scales[g][:, w],
+                    rhs=s_codes[g][:, c, cols].bitcast(FP8X4),
+                    rhs_scale=s_scales[g][:, c, cols],
+                    start=(c == 0),
+                    stop=(c == 1),
+                )
+            nc.scalar.copy(out=taps[(g, xh)][:, KT - 1, cols], in_=acc[:])
+
+        def new_z(g):
+            for xh in range(2):
+                z_grp[(g, xh)] = zgrp_pool.tile(
+                    [P, N, KT], BF16, name="z_grp", tag="z_grp", align_bytes=64
+                )
+                z_codes[(g, xh)] = zcode_pool.tile(
+                    [P, N], U32, name="z_codes", tag="z_codes", align_bytes=64
+                )
+                z_scales[(g, xh)] = zcode_pool.tile(
+                    [P, N], U8, name="z_scales", tag="z_scales", align_bytes=64
+                )
+
+        def z_split(g, lo, hi):
+            return lo + (hi - lo) * V_COLS_Z[g] // N
+
+        def regroup_z_scalar(g, xh, lo, hi):
+            regroup(z_grp[(g, xh)], taps[(g, xh)], z_split(g, lo, hi), hi, nc.scalar.copy)
+
+        def regroup_z_vector(g, xh, lo, hi):
+            regroup(z_grp[(g, xh)], taps[(g, xh)], lo, z_split(g, lo, hi), nc.vector.tensor_copy)
+
+        def quant_z(g, xh, lo, hi):
+            nc.vector.quantize_mx(
+                out=z_codes[(g, xh)][:, lo:hi].bitcast(FP8X4),
+                scales=z_scales[(g, xh)][:, lo:hi],
+                in_=z_grp[(g, xh)][:, lo:hi, :].rearrange("p n t -> p (n t)"),
+            )
+
+        def combine(g, nh):
+            cols = slice(nh * HALF, (nh + 1) * HALF)
+            acc2[(g, nh)] = ps_2.tile([P, HALF], F32, name="acc2", tag="acc2")
+            for xh in range(2):
+                w = slice(xh * P, (xh + 1) * P)
+                nc.tensor.matmul_mx(
+                    out=acc2[(g, nh)][:],
+                    lhsT=w_codes[:, w].bitcast(FP8X4),
+                    lhsT_scale=w_scales[:, w],
+                    rhs=z_codes[(g, xh)][:, cols].bitcast(FP8X4),
+                    rhs_scale=z_scales[(g, xh)][:, cols],
+                    start=(xh == 0),
+                    stop=(xh == 1),
+                )
+
+        o_sb = {}
+
+        def finish(g, nh):
+            if nh == 0:
+                o_sb[g] = out_pool.tile([P, N], F32, name="o_sb", tag="o_sb")
+            cols = slice(nh * HALF, (nh + 1) * HALF)
+            nc.scalar.activation(
+                out=o_sb[g][:, cols], in_=acc2[(g, nh)][:], func=RELU, bias=bias[:, 0:1], scale=1.0
+            )
+
+        def store(g, lo, hi):
+            nc.scalar.dma_start(out=out[g][:, lo:hi], in_=o_sb[g][:, lo:hi])
+
+        load_s(0)
+        load_taps(0)
+        ident_f = const.tile([P, P], F32, name="ident_f")
+        make_identity(nc, ident_f[:])
+        ident_b = const.tile([P, P], BF16, name="ident_b")
+        make_identity(nc, ident_b[:])
+        w_raw = const.tile([P, 2, KT * G], BF16, name="w_raw")
+        nc.scalar.dma_start(out=w_raw[:, 0, :], in_=weight_A.rearrange("o t f -> o (t f)"))
+        nc.scalar.dma_start(out=w_raw[:, 1, :], in_=weight_B.rearrange("o t f -> o (t f)"))
+        b_rows = const.tile([P, P], BF16, name="b_rows")
+        nc.vector.memset(b_rows[:], 0.0)
+        nc.scalar.dma_start(out=b_rows[0:1, :], in_=bias_A.rearrange("g o -> o g"))
+        nc.scalar.dma_start(out=b_rows[1:2, :], in_=bias_B.rearrange("g o -> o g"))
+        load_s(1)
+        load_taps(1)
+        load_s(2)
+        load_taps(2)
+
+        w_grp = const.tile([P, 2, G, KT], BF16, name="w_grp", align_bytes=64)
+        w_codes = const.tile([P, 2 * G], U32, name="w_codes", align_bytes=64)
+        w_scales = const.tile([P, 2 * G], U8, name="w_scales", align_bytes=64)
+        b_cols = const.tile([P, 2], F32, name="b_cols")
+        bias = const.tile([P, 1], F32, name="bias")
+
+        def prepare_weights():
+            wt = ps_t.tile([P, 2, KT, G], BF16, name="wt", tag="tp")
+            for w in range(2):
+                for t in range(KT):
+                    nc.tensor.transpose(
+                        wt[:, w, t, :], w_raw[:, w, t * G : (t + 1) * G], ident_b[:]
+                    )
+            nc.vector.tensor_copy(out=w_grp[:], in_=wt[:].rearrange("p w t o -> p w o t"))
+            bt = ps_t.tile([P, P], BF16, name="bt", tag="tp")
+            nc.tensor.transpose(bt[:], b_rows[:], ident_b[:])
+            nc.vector.tensor_copy(out=b_cols[:], in_=bt[:, 0:2])
+            nc.vector.quantize_mx(
+                out=w_codes[:].bitcast(FP8X4),
+                scales=w_scales[:],
+                in_=w_grp[:].rearrange("p w o t -> p (w o t)"),
+            )
+            nc.vector.tensor_add(out=bias[:], in0=b_cols[:, 0:1], in1=b_cols[:, 1:2])
+
+        for i in range(-1, B - 1):
+            now = 0 <= i
+            if now:
+                shift(i, 0, 0)
+                shift(i, 0, 1)
+            regroup_s(i + 1, 0)
+            regroup_s(i + 1, 1)
+            if now:
+                new_z(i)
+                regroup_z_scalar(i, 0, 0, N)
+                shift(i, 1, 0)
+                shift(i, 1, 1)
+            if 1 <= i:
+                combine(i - 1, 0)
+                combine(i - 1, 1)
+            transpose_x2(i + 1)
+            quant_s(i + 1, 0)
+            if now:
+                regroup_z_vector(i, 0, 0, N)
+            quant_s(i + 1, 1)
+            if now:
+                regroup_z_scalar(i, 1, 0, N)
+                regroup_z_vector(i, 1, 0, N)
+            if 1 <= i:
+                finish(i - 1, 0)
+                finish(i - 1, 1)
+                store(i - 1, 0, N)
+            if i == -1:
+                prepare_weights()
+            quant_xt(i + 1)
+            if now:
+                quant_z(i, 0, 0, N)
+                quant_z(i, 1, 0, N)
+            if now and i + 3 < B:
+                load_s(i + 3)
+                load_taps(i + 3)
+
+        g = B - 1
+        new_z(g)
+        shift(g, 0, 0)
+        shift(g, 1, 0)
+        shift(g, 0, 1)
+        shift(g, 1, 1)
+        combine(g - 1, 0)
+        combine(g - 1, 1)
+        regroup_z_scalar(g, 0, 0, HALF)
+        regroup_z_vector(g, 0, 0, HALF)
+        regroup_z_scalar(g, 1, 0, HALF)
+        regroup_z_vector(g, 1, 0, HALF)
+        finish(g - 1, 0)
+        finish(g - 1, 1)
+        store(g - 1, 0, N)
+        regroup_z_vector(g, 0, HALF, N)
+        quant_z(g, 0, 0, HALF)
+        regroup_z_scalar(g, 0, HALF, N)
+        regroup_z_vector(g, 1, HALF, N)
+        quant_z(g, 1, 0, HALF)
+        regroup_z_scalar(g, 1, HALF, N)
+        combine(g, 0)
+        quant_z(g, 0, HALF, N)
+        quant_z(g, 1, HALF, N)
+        finish(g, 0)
+        store(g, 0, HALF)
+        combine(g, 1)
+        finish(g, 1)
+        store(g, HALF, N)

@@ -19,7 +19,7 @@ HALF = 512
 
 FLOPS = B * 2 * (2 * G * N * N + 2 * G * KT * G * N)
 
-MANUAL = True
+MANUAL = False
 V_COLS_S = [832, 960, 960, 1024, 1024, 1024, 1024, 1024]
 V_COLS_Z = [448, 320, 320, 320, 384, 320, 320, 832]
 

@@ -19,9 +19,9 @@ HALF = 512
 
 FLOPS = B * 2 * (2 * G * N * N + 2 * G * KT * G * N)
 
-MANUAL = False
-V_COLS_S = [832, 960, 960, 1024, 1024, 1024, 1024, 1024]
-V_COLS_Z = [448, 320, 320, 320, 384, 320, 320, 832]
+MANUAL = True
+V_COLS_S = [832, 960, 1024, 1024, 1024, 1024, 1024, 1024]
+V_COLS_Z = [320, 256, 256, 256, 256, 256, 256, 768]
 
 
 def tile_graphfilterrnnbatch_pb_kernel(
@@ -57,23 +57,31 @@ def tile_graphfilterrnnbatch_pb_kernel(
         z_scales = {}
         acc2 = {}
 
-        def load_s(g):
+        def new_inputs(g):
             s_raw[g] = sraw_pool.tile([P, 2, 4, N], BF16, name="s_raw", tag="s_raw")
-            for c in range(2):
-                nc.sync.dma_start(
-                    out=s_raw[g][:, c],
-                    in_=S[g, c * 512 : (c + 1) * 512, :].rearrange("(p j) m -> p j m", j=4),
-                )
-
-        def load_taps(g):
             for xh in range(2):
                 taps[(g, xh)] = taps_pool.tile(
                     [P, KT, N], BF16, name="taps%d" % xh, tag="taps%d" % xh
                 )
+
+        def load_s(g, c):
+            nc.sync.dma_start(
+                out=s_raw[g][:, c],
+                in_=S[g, c * 512 : (c + 1) * 512, :].rearrange("(p j) m -> p j m", j=4),
+            )
+
+        def load_taps(g, t_lo, t_hi):
+            for xh in range(2):
                 nc.sync.dma_start(
-                    out=taps[(g, xh)][:, 0 : KT - 1, :],
-                    in_=taps_in[xh][g].rearrange("t f n -> f t n"),
+                    out=taps[(g, xh)][:, t_lo:t_hi, :],
+                    in_=taps_in[xh][g, t_lo:t_hi].rearrange("t f n -> f t n"),
                 )
+
+        def load_graph(g):
+            new_inputs(g)
+            load_s(g, 0)
+            load_s(g, 1)
+            load_taps(g, 0, KT - 1)
 
         def regroup(dst, src, lo, hi, engine_copy):
             engine_copy(
@@ -197,25 +205,26 @@ def tile_graphfilterrnnbatch_pb_kernel(
             )
 
         def store(g, lo, hi):
-            nc.scalar.dma_start(out=out[g][:, lo:hi], in_=o_sb[g][:, lo:hi])
+            nc.sync.dma_start(out=out[g][:, lo:hi], in_=o_sb[g][:, lo:hi])
 
-        load_s(0)
-        load_taps(0)
+        new_inputs(0)
+        load_s(0, 0)
+        load_taps(0, KT - 2, KT - 1)
+        load_s(0, 1)
+        load_taps(0, 0, KT - 2)
         ident_f = const.tile([P, P], F32, name="ident_f")
         make_identity(nc, ident_f[:])
         ident_b = const.tile([P, P], BF16, name="ident_b")
         make_identity(nc, ident_b[:])
-        w_raw = const.tile([P, 2, KT * G], BF16, name="w_raw")
-        nc.scalar.dma_start(out=w_raw[:, 0, :], in_=weight_A.rearrange("o t f -> o (t f)"))
-        nc.scalar.dma_start(out=w_raw[:, 1, :], in_=weight_B.rearrange("o t f -> o (t f)"))
         b_rows = const.tile([P, P], BF16, name="b_rows")
         nc.vector.memset(b_rows[:], 0.0)
-        nc.scalar.dma_start(out=b_rows[0:1, :], in_=bias_A.rearrange("g o -> o g"))
-        nc.scalar.dma_start(out=b_rows[1:2, :], in_=bias_B.rearrange("g o -> o g"))
-        load_s(1)
-        load_taps(1)
-        load_s(2)
-        load_taps(2)
+        load_graph(1)
+        w_raw = const.tile([P, 2, KT * G], BF16, name="w_raw")
+        nc.sync.dma_start(out=w_raw[:, 0, :], in_=weight_A.rearrange("o t f -> o (t f)"))
+        nc.sync.dma_start(out=w_raw[:, 1, :], in_=weight_B.rearrange("o t f -> o (t f)"))
+        nc.sync.dma_start(out=b_rows[0:1, :], in_=bias_A.rearrange("g o -> o g"))
+        nc.sync.dma_start(out=b_rows[1:2, :], in_=bias_B.rearrange("g o -> o g"))
+        load_graph(2)
 
         w_grp = const.tile([P, 2, G, KT], BF16, name="w_grp", align_bytes=64)
         w_codes = const.tile([P, 2 * G], U32, name="w_codes", align_bytes=64)
@@ -223,17 +232,19 @@ def tile_graphfilterrnnbatch_pb_kernel(
         b_cols = const.tile([P, 2], F32, name="b_cols")
         bias = const.tile([P, 1], F32, name="bias")
 
-        def prepare_weights():
+        def transpose_weights():
             wt = ps_t.tile([P, 2, KT, G], BF16, name="wt", tag="tp")
             for w in range(2):
                 for t in range(KT):
                     nc.tensor.transpose(
                         wt[:, w, t, :], w_raw[:, w, t * G : (t + 1) * G], ident_b[:]
                     )
-            nc.vector.tensor_copy(out=w_grp[:], in_=wt[:].rearrange("p w t o -> p w o t"))
+            nc.scalar.copy(out=w_grp[:], in_=wt[:].rearrange("p w t o -> p w o t"))
             bt = ps_t.tile([P, P], BF16, name="bt", tag="tp")
             nc.tensor.transpose(bt[:], b_rows[:], ident_b[:])
-            nc.vector.tensor_copy(out=b_cols[:], in_=bt[:, 0:2])
+            nc.scalar.copy(out=b_cols[:], in_=bt[:, 0:2])
+
+        def quant_weights():
             nc.vector.quantize_mx(
                 out=w_codes[:].bitcast(FP8X4),
                 scales=w_scales[:],
@@ -241,8 +252,14 @@ def tile_graphfilterrnnbatch_pb_kernel(
             )
             nc.vector.tensor_add(out=bias[:], in0=b_cols[:, 0:1], in1=b_cols[:, 1:2])
 
-        for i in range(-1, B - 1):
-            now = 0 <= i
+        regroup_s(0, 0)
+        transpose_x2(0)
+        quant_s(0, 0)
+        regroup_s(0, 1)
+        quant_xt(0)
+        quant_s(0, 1)
+        for i in range(B - 1):
+            now = True
             if now:
                 shift(i, 0, 0)
                 shift(i, 0, 1)
@@ -268,15 +285,16 @@ def tile_graphfilterrnnbatch_pb_kernel(
                 finish(i - 1, 0)
                 finish(i - 1, 1)
                 store(i - 1, 0, N)
-            if i == -1:
-                prepare_weights()
+            if i == 0:
+                transpose_weights()
             quant_xt(i + 1)
             if now:
                 quant_z(i, 0, 0, N)
                 quant_z(i, 1, 0, N)
-            if now and i + 3 < B:
-                load_s(i + 3)
-                load_taps(i + 3)
+            if i == 0:
+                quant_weights()
+            if i + 3 < B:
+                load_graph(i + 3)
 
         g = B - 1
         new_z(g)

@@ -21,7 +21,7 @@ FLOPS = B * 2 * (2 * G * N * N + 2 * G * KT * G * N)
 
 MANUAL = True
 V_COLS_S = [832, 960, 1024, 1024, 1024, 1024, 1024, 1024]
-V_COLS_Z = [320, 256, 256, 256, 256, 256, 256, 768]
+V_COLS_Z = [352, 288, 288, 288, 288, 288, 288, 768]
 
 
 def tile_graphfilterrnnbatch_pb_kernel(

@@ -19,9 +19,9 @@ HALF = 512
 
 FLOPS = B * 2 * (2 * G * N * N + 2 * G * KT * G * N)
 
-MANUAL = True
 V_COLS_S = [832, 960, 1024, 1024, 1024, 1024, 1024, 1024]
-V_COLS_Z = [352, 288, 288, 288, 288, 288, 288, 768]
+V_COLS_Z = [304, 240, 240, 240, 240, 240, 240, 768]
+PE_COLS_Z = 256
 
 
 def tile_graphfilterrnnbatch_pb_kernel(
@@ -40,10 +40,10 @@ def tile_graphfilterrnnbatch_pb_kernel(
         xt_pool = ctx.enter_context(tc.tile_pool(name="xt", bufs=2))
         out_pool = ctx.enter_context(tc.tile_pool(name="outp", bufs=3))
         ps_t = ctx.enter_context(tc.psum_pool(name="ps_t", bufs=2))
-        ps_1 = ctx.enter_context(tc.psum_pool(name="ps_1", bufs=4))
+        ps_1 = ctx.enter_context(tc.psum_pool(name="ps_1", bufs=3))
+        ps_i = ctx.enter_context(tc.psum_pool(name="ps_i", bufs=1))
         ps_2 = ctx.enter_context(tc.psum_pool(name="ps_2", bufs=2))
-        if MANUAL:
-            ctx.enter_context(tc.manual_schedule())
+        ctx.enter_context(tc.manual_schedule())
 
         s_raw = {}
         s_codes = {}
@@ -172,6 +172,25 @@ def tile_graphfilterrnnbatch_pb_kernel(
         def regroup_z_vector(g, xh, lo, hi):
             regroup(z_grp[(g, xh)], taps[(g, xh)], lo, z_split(g, lo, hi), nc.vector.tensor_copy)
 
+        def interleave_z(g, xh):
+            acc = ps_i.tile([P, PE_COLS_Z, KT], BF16, name="acc_i", tag="acc_i")
+            for b in range(PE_COLS_Z // P):
+                lo = N - PE_COLS_Z + b * P
+                nc.tensor.matmul(
+                    acc[:, b * P : (b + 1) * P, :],
+                    ident_b[:],
+                    taps[(g, xh)][:, :, lo : lo + P].rearrange("f t n -> f n t"),
+                    start=True,
+                    stop=True,
+                )
+            return acc
+
+        def copy_interleaved(g, xh, acc):
+            nc.scalar.copy(
+                out=z_grp[(g, xh)][:, N - PE_COLS_Z : N, :].rearrange("p n t -> p (n t)").bitcast(F32),
+                in_=acc[:].rearrange("p n t -> p (n t)").bitcast(F32),
+            )
+
         def quant_z(g, xh, lo, hi):
             nc.vector.quantize_mx(
                 out=z_codes[(g, xh)][:, lo:hi].bitcast(FP8X4),
@@ -259,28 +278,27 @@ def tile_graphfilterrnnbatch_pb_kernel(
         quant_xt(0)
         quant_s(0, 1)
         for i in range(B - 1):
-            now = True
-            if now:
-                shift(i, 0, 0)
-                shift(i, 0, 1)
+            shift(i, 0, 0)
+            shift(i, 0, 1)
             regroup_s(i + 1, 0)
             regroup_s(i + 1, 1)
-            if now:
-                new_z(i)
-                regroup_z_scalar(i, 0, 0, N)
-                shift(i, 1, 0)
-                shift(i, 1, 1)
+            new_z(i)
+            regroup(z_grp[(i, 0)], taps[(i, 0)], V_COLS_Z[i], N - PE_COLS_Z, nc.scalar.copy)
+            shift(i, 1, 0)
+            shift(i, 1, 1)
             if 1 <= i:
                 combine(i - 1, 0)
                 combine(i - 1, 1)
+            acc = interleave_z(i, 0)
             transpose_x2(i + 1)
+            copy_interleaved(i, 0, acc)
+            acc = interleave_z(i, 1)
             quant_s(i + 1, 0)
-            if now:
-                regroup_z_vector(i, 0, 0, N)
+            regroup(z_grp[(i, 0)], taps[(i, 0)], 0, V_COLS_Z[i], nc.vector.tensor_copy)
             quant_s(i + 1, 1)
-            if now:
-                regroup_z_scalar(i, 1, 0, N)
-                regroup_z_vector(i, 1, 0, N)
+            regroup(z_grp[(i, 1)], taps[(i, 1)], V_COLS_Z[i], N - PE_COLS_Z, nc.scalar.copy)
+            regroup(z_grp[(i, 1)], taps[(i, 1)], 0, V_COLS_Z[i], nc.vector.tensor_copy)
+            copy_interleaved(i, 1, acc)
             if 1 <= i:
                 finish(i - 1, 0)
                 finish(i - 1, 1)
@@ -288,9 +306,8 @@ def tile_graphfilterrnnbatch_pb_kernel(
             if i == 0:
                 transpose_weights()
             quant_xt(i + 1)
-            if now:
-                quant_z(i, 0, 0, N)
-                quant_z(i, 1, 0, N)
+            quant_z(i, 0, 0, N)
+            quant_z(i, 1, 0, N)
             if i == 0:
                 quant_weights()
             if i + 3 < B:

@@ -85,8 +85,8 @@ def tile_graphfilterrnnbatch_pb_kernel(
 
         def regroup(dst, src, lo, hi, engine_copy):
             engine_copy(
-                out=dst[:, lo:hi, :].rearrange("p (c i) t -> p c t i", i=4),
-                in_=src[:, :, lo:hi].rearrange("p t (c i) -> p c t i", i=4),
+                out=dst[:, lo:hi, :].rearrange("p (c i) t -> p c t i", i=8),
+                in_=src[:, :, lo:hi].rearrange("p t (c i) -> p c t i", i=8),
             )
 
         s_grp = {}

@@ -19,9 +19,11 @@ HALF = 512
 
 FLOPS = B * 2 * (2 * G * N * N + 2 * G * KT * G * N)
 
-V_COLS_S = [832, 960, 1024, 1024, 1024, 1024, 1024, 1024]
-V_COLS_Z = [304, 240, 240, 240, 240, 240, 240, 768]
+V_HALF_S0 = 336
+V_COLS_S = [N, 1024, N, N, N, N, N, N]
+V_COLS_Z = [352, 224, 224, 224, 224, 224, 224, 576]
 PE_COLS_Z = 256
+PE_LO_Z = 768
 
 
 def tile_graphfilterrnnbatch_pb_kernel(
@@ -31,7 +33,7 @@ def tile_graphfilterrnnbatch_pb_kernel(
     taps_in = [x_taps, h_taps]
     with ExitStack() as ctx:
         const = ctx.enter_context(tc.tile_pool(name="const", bufs=1))
-        sraw_pool = ctx.enter_context(tc.tile_pool(name="sraw", bufs=3))
+        sraw_pool = ctx.enter_context(tc.tile_pool(name="sraw", bufs=6))
         sgrp_pool = ctx.enter_context(tc.tile_pool(name="sgrp", bufs=3))
         scode_pool = ctx.enter_context(tc.tile_pool(name="scode", bufs=2))
         taps_pool = ctx.enter_context(tc.tile_pool(name="taps", bufs=3))
@@ -58,7 +60,9 @@ def tile_graphfilterrnnbatch_pb_kernel(
         acc2 = {}
 
         def new_inputs(g):
-            s_raw[g] = sraw_pool.tile([P, 2, 4, N], BF16, name="s_raw", tag="s_raw")
+            for c in range(2):
+                shape = [P, 4, N] if g else [P, 2, 4, HALF]
+                s_raw[(g, c)] = sraw_pool.tile(shape, BF16, name="s_raw", tag="s_raw")
             for xh in range(2):
                 taps[(g, xh)] = taps_pool.tile(
                     [P, KT, N], BF16, name="taps%d" % xh, tag="taps%d" % xh
@@ -66,8 +70,16 @@ def tile_graphfilterrnnbatch_pb_kernel(
 
         def load_s(g, c):
             nc.sync.dma_start(
-                out=s_raw[g][:, c],
+                out=s_raw[(g, c)][:],
                 in_=S[g, c * 512 : (c + 1) * 512, :].rearrange("(p j) m -> p j m", j=4),
+            )
+
+        def load_s_half(c, h):
+            nc.sync.dma_start(
+                out=s_raw[(0, c)][:, h],
+                in_=S[0, c * 512 : (c + 1) * 512, h * HALF : (h + 1) * HALF].rearrange(
+                    "(p j) m -> p j m", j=4
+                ),
             )
 
         def load_taps(g, t_lo, t_hi):
@@ -91,13 +103,21 @@ def tile_graphfilterrnnbatch_pb_kernel(
 
         s_grp = {}
 
-        def regroup_s(g, c):
+        def new_s_grp(g, c):
             s_grp[(g, c)] = sgrp_pool.tile(
                 [P, N, 4], BF16, name="s_grp", tag="s_grp", align_bytes=64
             )
-            regroup(s_grp[(g, c)], s_raw[g][:, c], 0, V_COLS_S[g], nc.vector.tensor_copy)
+
+        def regroup_s_half(c, h):
+            dst = s_grp[(0, c)][:, h * HALF : (h + 1) * HALF, :]
+            regroup(dst, s_raw[(0, c)][:, h], 0, V_HALF_S0, nc.vector.tensor_copy)
+            regroup(dst, s_raw[(0, c)][:, h], V_HALF_S0, HALF, nc.scalar.copy)
+
+        def regroup_s(g, c):
+            new_s_grp(g, c)
+            regroup(s_grp[(g, c)], s_raw[(g, c)], 0, V_COLS_S[g], nc.vector.tensor_copy)
             if V_COLS_S[g] < N:
-                regroup(s_grp[(g, c)], s_raw[g][:, c], V_COLS_S[g], N, nc.scalar.copy)
+                regroup(s_grp[(g, c)], s_raw[(g, c)], V_COLS_S[g], N, nc.scalar.copy)
 
         def quant_s(g, c):
             if c == 0:
@@ -135,9 +155,9 @@ def tile_graphfilterrnnbatch_pb_kernel(
                 out=xt_codes[g][:].bitcast(FP8X4), scales=xt_scales[g][:], in_=xt_grp[g][:]
             )
 
-        def shift(g, xh, mh):
+        def shift_mm(g, xh, mh, pool, tag):
             cols = slice(mh * HALF, (mh + 1) * HALF)
-            acc = ps_1.tile([P, HALF], F32, name="acc1", tag="acc1")
+            acc = pool.tile([P, HALF], F32, name="acc1", tag=tag)
             for c in range(2):
                 w = slice((xh * 2 + c) * P, (xh * 2 + c + 1) * P)
                 nc.tensor.matmul_mx(
@@ -149,7 +169,15 @@ def tile_graphfilterrnnbatch_pb_kernel(
                     start=(c == 0),
                     stop=(c == 1),
                 )
-            nc.scalar.copy(out=taps[(g, xh)][:, KT - 1, cols], in_=acc[:])
+            return acc
+
+        def copy_shift(g, xh, mh, acc, engine_copy):
+            cols = slice(mh * HALF, (mh + 1) * HALF)
+            engine_copy(out=taps[(g, xh)][:, KT - 1, cols], in_=acc[:])
+
+        def shift(g, xh, mh):
+            acc = shift_mm(g, xh, mh, ps_1, "acc1")
+            copy_shift(g, xh, mh, acc, nc.scalar.copy)
 
         def new_z(g):
             for xh in range(2):
@@ -163,31 +191,22 @@ def tile_graphfilterrnnbatch_pb_kernel(
                     [P, N], U8, name="z_scales", tag="z_scales", align_bytes=64
                 )
 
-        def z_split(g, lo, hi):
-            return lo + (hi - lo) * V_COLS_Z[g] // N
-
-        def regroup_z_scalar(g, xh, lo, hi):
-            regroup(z_grp[(g, xh)], taps[(g, xh)], z_split(g, lo, hi), hi, nc.scalar.copy)
-
-        def regroup_z_vector(g, xh, lo, hi):
-            regroup(z_grp[(g, xh)], taps[(g, xh)], lo, z_split(g, lo, hi), nc.vector.tensor_copy)
-
-        def interleave_z(g, xh):
-            acc = ps_i.tile([P, PE_COLS_Z, KT], BF16, name="acc_i", tag="acc_i")
+        def interleave_z(g, xh, lo, pool, tag):
+            acc = pool.tile([P, PE_COLS_Z, KT], BF16, name="acc_i", tag=tag)
             for b in range(PE_COLS_Z // P):
-                lo = N - PE_COLS_Z + b * P
+                cols = slice(lo + b * P, lo + (b + 1) * P)
                 nc.tensor.matmul(
                     acc[:, b * P : (b + 1) * P, :],
                     ident_b[:],
-                    taps[(g, xh)][:, :, lo : lo + P].rearrange("f t n -> f n t"),
+                    taps[(g, xh)][:, :, cols].rearrange("f t n -> f n t"),
                     start=True,
                     stop=True,
                 )
             return acc
 
-        def copy_interleaved(g, xh, acc):
-            nc.scalar.copy(
-                out=z_grp[(g, xh)][:, N - PE_COLS_Z : N, :].rearrange("p n t -> p (n t)").bitcast(F32),
+        def copy_interleaved(g, xh, lo, acc, engine_copy):
+            engine_copy(
+                out=z_grp[(g, xh)][:, lo : lo + PE_COLS_Z, :].rearrange("p n t -> p (n t)").bitcast(F32),
                 in_=acc[:].rearrange("p n t -> p (n t)").bitcast(F32),
             )
 
@@ -227,17 +246,23 @@ def tile_graphfilterrnnbatch_pb_kernel(
             nc.sync.dma_start(out=out[g][:, lo:hi], in_=o_sb[g][:, lo:hi])
 
         new_inputs(0)
-        load_s(0, 0)
+        load_s_half(0, 0)
+        load_s_half(0, 1)
         load_taps(0, KT - 2, KT - 1)
-        load_s(0, 1)
+        load_s_half(1, 0)
+        load_s_half(1, 1)
+        new_inputs(1)
+        load_s(1, 0)
+        load_s(1, 1)
         load_taps(0, 0, KT - 2)
+        load_taps(1, KT - 2, KT - 1)
+        load_taps(1, 0, KT - 2)
         ident_f = const.tile([P, P], F32, name="ident_f")
         make_identity(nc, ident_f[:])
         ident_b = const.tile([P, P], BF16, name="ident_b")
         make_identity(nc, ident_b[:])
         b_rows = const.tile([P, P], BF16, name="b_rows")
         nc.vector.memset(b_rows[:], 0.0)
-        load_graph(1)
         w_raw = const.tile([P, 2, KT * G], BF16, name="w_raw")
         nc.sync.dma_start(out=w_raw[:, 0, :], in_=weight_A.rearrange("o t f -> o (t f)"))
         nc.sync.dma_start(out=w_raw[:, 1, :], in_=weight_B.rearrange("o t f -> o (t f)"))
@@ -271,74 +296,90 @@ def tile_graphfilterrnnbatch_pb_kernel(
             )
             nc.vector.tensor_add(out=bias[:], in0=b_cols[:, 0:1], in1=b_cols[:, 1:2])
 
-        regroup_s(0, 0)
+        new_s_grp(0, 0)
+        new_s_grp(0, 1)
+        regroup_s_half(0, 0)
+        regroup_s_half(0, 1)
         transpose_x2(0)
         quant_s(0, 0)
-        regroup_s(0, 1)
+        regroup_s_half(1, 0)
+        regroup_s_half(1, 1)
         quant_xt(0)
         quant_s(0, 1)
         for i in range(B - 1):
             shift(i, 0, 0)
             shift(i, 0, 1)
             regroup_s(i + 1, 0)
+            if 1 <= i:
+                quant_z(i - 1, 0, 0, N)
             regroup_s(i + 1, 1)
+            if i == 1:
+                quant_weights()
+            if 1 <= i:
+                quant_z(i - 1, 1, 0, N)
             new_z(i)
-            regroup(z_grp[(i, 0)], taps[(i, 0)], V_COLS_Z[i], N - PE_COLS_Z, nc.scalar.copy)
+            regroup(z_grp[(i, 0)], taps[(i, 0)], V_COLS_Z[i], PE_LO_Z, nc.scalar.copy)
+            transpose_x2(i + 1)
             shift(i, 1, 0)
             shift(i, 1, 1)
-            if 1 <= i:
-                combine(i - 1, 0)
-                combine(i - 1, 1)
-            acc = interleave_z(i, 0)
-            transpose_x2(i + 1)
-            copy_interleaved(i, 0, acc)
-            acc = interleave_z(i, 1)
+            acc = interleave_z(i, 0, PE_LO_Z, ps_i, "acc_i")
             quant_s(i + 1, 0)
             regroup(z_grp[(i, 0)], taps[(i, 0)], 0, V_COLS_Z[i], nc.vector.tensor_copy)
             quant_s(i + 1, 1)
-            regroup(z_grp[(i, 1)], taps[(i, 1)], V_COLS_Z[i], N - PE_COLS_Z, nc.scalar.copy)
+            if 1 <= i:
+                combine(i - 1, 0)
+                combine(i - 1, 1)
+            copy_interleaved(i, 0, PE_LO_Z, acc, nc.scalar.copy)
+            acc = interleave_z(i, 1, PE_LO_Z, ps_i, "acc_i")
+            regroup(z_grp[(i, 1)], taps[(i, 1)], V_COLS_Z[i], PE_LO_Z, nc.scalar.copy)
             regroup(z_grp[(i, 1)], taps[(i, 1)], 0, V_COLS_Z[i], nc.vector.tensor_copy)
-            copy_interleaved(i, 1, acc)
             if 1 <= i:
                 finish(i - 1, 0)
                 finish(i - 1, 1)
                 store(i - 1, 0, N)
             if i == 0:
                 transpose_weights()
+            copy_interleaved(i, 1, PE_LO_Z, acc, nc.scalar.copy)
             quant_xt(i + 1)
-            quant_z(i, 0, 0, N)
-            quant_z(i, 1, 0, N)
-            if i == 0:
-                quant_weights()
             if i + 3 < B:
                 load_graph(i + 3)
 
         g = B - 1
+        v_copy = nc.vector.tensor_copy
+        s_copy = nc.scalar.copy
         new_z(g)
-        shift(g, 0, 0)
-        shift(g, 1, 0)
-        shift(g, 0, 1)
-        shift(g, 1, 1)
+        halves = [slice(0, HALF), slice(HALF, N)]
+        split = [nh * HALF + V_COLS_Z[g] // 2 for nh in range(2)]
+        a0 = shift_mm(g, 0, 0, ps_1, "acc1")
+        a1 = shift_mm(g, 1, 0, ps_1, "acc1")
+        a2 = shift_mm(g, 0, 1, ps_1, "acc1")
+        a3 = shift_mm(g, 1, 1, ps_t, "tp")
+        quant_z(g - 1, 0, 0, N)
+        copy_shift(g, 0, 0, a0, v_copy)
+        copy_shift(g, 1, 0, a1, v_copy)
+        regroup(z_grp[(g, 0)], taps[(g, 0)], 0, split[0], v_copy)
+        quant_z(g - 1, 1, 0, N)
+        copy_shift(g, 0, 1, a2, s_copy)
+        copy_shift(g, 1, 1, a3, s_copy)
         combine(g - 1, 0)
         combine(g - 1, 1)
-        regroup_z_scalar(g, 0, 0, HALF)
-        regroup_z_vector(g, 0, 0, HALF)
-        regroup_z_scalar(g, 1, 0, HALF)
-        regroup_z_vector(g, 1, 0, HALF)
+        regroup(z_grp[(g, 0)], taps[(g, 0)], split[0], HALF, s_copy)
+        regroup(z_grp[(g, 1)], taps[(g, 1)], split[0], HALF, s_copy)
+        regroup(z_grp[(g, 1)], taps[(g, 1)], 0, split[0], v_copy)
         finish(g - 1, 0)
+        quant_z(g, 0, 0, HALF)
+        regroup(z_grp[(g, 0)], taps[(g, 0)], split[1], N, s_copy)
+        regroup(z_grp[(g, 0)], taps[(g, 0)], HALF, split[1], v_copy)
+        quant_z(g, 1, 0, HALF)
+        regroup(z_grp[(g, 1)], taps[(g, 1)], HALF, split[1], v_copy)
+        regroup(z_grp[(g, 1)], taps[(g, 1)], split[1], N, s_copy)
         finish(g - 1, 1)
         store(g - 1, 0, N)
-        regroup_z_vector(g, 0, HALF, N)
-        quant_z(g, 0, 0, HALF)
-        regroup_z_scalar(g, 0, HALF, N)
-        regroup_z_vector(g, 1, HALF, N)
-        quant_z(g, 1, 0, HALF)
-        regroup_z_scalar(g, 1, HALF, N)
-        combine(g, 0)
         quant_z(g, 0, HALF, N)
-        quant_z(g, 1, HALF, N)
+        combine(g, 0)
         finish(g, 0)
         store(g, 0, HALF)
+        quant_z(g, 1, HALF, N)
         combine(g, 1)
         finish(g, 1)
         store(g, HALF, N)

from contextlib import ExitStack

import concourse.mybir as mybir
from concourse.masks import make_identity

FP8X4 = mybir.dt.float8_e4m3fn_x4
BF16 = mybir.dt.bfloat16
F32 = mybir.dt.float32
U32 = mybir.dt.uint32
U8 = mybir.dt.uint8
RELU = mybir.ActivationFunctionType.Relu

B = 8
N = 1024
G = 128
KT = 4
P = 128
HALF = 512

FLOPS = B * 2 * (2 * G * N * N + 2 * G * KT * G * N)

V_HALF_S0 = 336
V_COLS_S = [N, 1024, N, N, N, N, N, N]
V_COLS_Z = [352, 224, 224, 224, 224, 224, 224, 576]
PE_COLS_Z = 256
PE_LO_Z = 768


def tile_graphfilterrnnbatch_pb_kernel(
    tc, x_taps, h_taps, S, weight_A, weight_B, bias_A, bias_B, out
):
    nc = tc.nc
    taps_in = [x_taps, h_taps]
    with ExitStack() as ctx:
        const = ctx.enter_context(tc.tile_pool(name="const", bufs=1))
        sraw_pool = ctx.enter_context(tc.tile_pool(name="sraw", bufs=6))
        sgrp_pool = ctx.enter_context(tc.tile_pool(name="sgrp", bufs=3))
        scode_pool = ctx.enter_context(tc.tile_pool(name="scode", bufs=2))
        taps_pool = ctx.enter_context(tc.tile_pool(name="taps", bufs=3))
        zgrp_pool = ctx.enter_context(tc.tile_pool(name="zgrp", bufs=4))
        zcode_pool = ctx.enter_context(tc.tile_pool(name="zcode", bufs=4))
        xt_pool = ctx.enter_context(tc.tile_pool(name="xt", bufs=2))
        out_pool = ctx.enter_context(tc.tile_pool(name="outp", bufs=3))
        ps_t = ctx.enter_context(tc.psum_pool(name="ps_t", bufs=2))
        ps_1 = ctx.enter_context(tc.psum_pool(name="ps_1", bufs=3))
        ps_i = ctx.enter_context(tc.psum_pool(name="ps_i", bufs=1))
        ps_2 = ctx.enter_context(tc.psum_pool(name="ps_2", bufs=2))
        ctx.enter_context(tc.manual_schedule())

        s_raw = {}
        s_codes = {}
        s_scales = {}
        taps = {}
        xt_grp = {}
        xt_codes = {}
        xt_scales = {}
        z_grp = {}
        z_codes = {}
        z_scales = {}
        acc2 = {}

        def new_inputs(g):
            for c in range(2):
                shape = [P, 4, N] if g else [P, 2, 4, HALF]
                s_raw[(g, c)] = sraw_pool.tile(shape, BF16, name="s_raw", tag="s_raw")
            for xh in range(2):
                taps[(g, xh)] = taps_pool.tile(
                    [P, KT, N], BF16, name="taps%d" % xh, tag="taps%d" % xh
                )

        def load_s(g, c):
            nc.sync.dma_start(
                out=s_raw[(g, c)][:],
                in_=S[g, c * 512 : (c + 1) * 512, :].rearrange("(p j) m -> p j m", j=4),
            )

        def load_s_half(c, h):
            nc.sync.dma_start(
                out=s_raw[(0, c)][:, h],
                in_=S[0, c * 512 : (c + 1) * 512, h * HALF : (h + 1) * HALF].rearrange(
                    "(p j) m -> p j m", j=4
                ),
            )

        def load_taps(g, t_lo, t_hi):
            for xh in range(2):
                nc.sync.dma_start(
                    out=taps[(g, xh)][:, t_lo:t_hi, :],
                    in_=taps_in[xh][g, t_lo:t_hi].rearrange("t f n -> f t n"),
                )

        def load_graph(g):
            new_inputs(g)
            load_s(g, 0)
            load_s(g, 1)
            load_taps(g, 0, KT - 1)

        def regroup(dst, src, lo, hi, engine_copy):
            engine_copy(
                out=dst[:, lo:hi, :].rearrange("p (c i) t -> p c t i", i=8),
                in_=src[:, :, lo:hi].rearrange("p t (c i) -> p c t i", i=8),
            )

        s_grp = {}

        def new_s_grp(g, c):
            s_grp[(g, c)] = sgrp_pool.tile(
                [P, N, 4], BF16, name="s_grp", tag="s_grp", align_bytes=64
            )

        def regroup_s_half(c, h):
            dst = s_grp[(0, c)][:, h * HALF : (h + 1) * HALF, :]
            regroup(dst, s_raw[(0, c)][:, h], 0, V_HALF_S0, nc.vector.tensor_copy)
            regroup(dst, s_raw[(0, c)][:, h], V_HALF_S0, HALF, nc.scalar.copy)

        def regroup_s(g, c):
            new_s_grp(g, c)
            regroup(s_grp[(g, c)], s_raw[(g, c)], 0, V_COLS_S[g], nc.vector.tensor_copy)
            if V_COLS_S[g] < N:
                regroup(s_grp[(g, c)], s_raw[(g, c)], V_COLS_S[g], N, nc.scalar.copy)

        def quant_s(g, c):
            if c == 0:
                s_codes[g] = scode_pool.tile(
                    [P, 2, N], U32, name="s_codes", tag="s_codes", align_bytes=64
                )
                s_scales[g] = scode_pool.tile(
                    [P, 2, N], U8, name="s_scales", tag="s_scales", align_bytes=64
                )
            nc.vector.quantize_mx(
                out=s_codes[g][:, c, :].bitcast(FP8X4),
                scales=s_scales[g][:, c, :],
                in_=s_grp[(g, c)][:].rearrange("p m j -> p (m j)"),
            )

        def transpose_x2(g):
            xt_grp[g] = xt_pool.tile([P, 4 * 512], BF16, name="xt_grp", tag="xt_grp", align_bytes=64)
            dst = xt_grp[g][:].bitcast(F32).rearrange("p (x c f u) -> p x c f u", x=2, c=2, u=2)
            for xh in range(2):
                tp = ps_t.tile([P, 2, 2, P], F32, name="tp", tag="tp")
                words = (
                    taps[(g, xh)][:, KT - 2, :]
                    .bitcast(F32)
                    .rearrange("f (c p u) -> f c u p", c=2, u=2)
                )
                for c in range(2):
                    for u in range(2):
                        nc.tensor.transpose(tp[:, c, u, :], words[:, c, u, :], ident_f[:])
                nc.scalar.copy(out=dst[:, xh], in_=tp[:].rearrange("p c u f -> p c f u"))

        def quant_xt(g):
            xt_codes[g] = xt_pool.tile([P, 512], U32, name="xt_codes", tag="xt_codes", align_bytes=64)
            xt_scales[g] = xt_pool.tile([P, 512], U8, name="xt_scales", tag="xt_scales", align_bytes=64)
            nc.vector.quantize_mx(
                out=xt_codes[g][:].bitcast(FP8X4), scales=xt_scales[g][:], in_=xt_grp[g][:]
            )

        def shift_mm(g, xh, mh, pool, tag):
            cols = slice(mh * HALF, (mh + 1) * HALF)
            acc = pool.tile([P, HALF], F32, name="acc1", tag=tag)
            for c in range(2):
                w = slice((xh * 2 + c) * P, (xh * 2 + c + 1) * P)
                nc.tensor.matmul_mx(
                    out=acc[:],
                    lhsT=xt_codes[g][:, w].bitcast(FP8X4),
                    lhsT_scale=xt_scales[g][:, w],
                    rhs=s_codes[g][:, c, cols].bitcast(FP8X4),
                    rhs_scale=s_scales[g][:, c, cols],
                    start=(c == 0),
                    stop=(c == 1),
                )
            return acc

        def copy_shift(g, xh, mh, acc, engine_copy):
            cols = slice(mh * HALF, (mh + 1) * HALF)
            engine_copy(out=taps[(g, xh)][:, KT - 1, cols], in_=acc[:])

        def shift(g, xh, mh):
            acc = shift_mm(g, xh, mh, ps_1, "acc1")
            copy_shift(g, xh, mh, acc, nc.scalar.copy)

        def new_z(g):
            for xh in range(2):
                z_grp[(g, xh)] = zgrp_pool.tile(
                    [P, N, KT], BF16, name="z_grp", tag="z_grp", align_bytes=64
                )
                z_codes[(g, xh)] = zcode_pool.tile(
                    [P, N], U32, name="z_codes", tag="z_codes", align_bytes=64
                )
                z_scales[(g, xh)] = zcode_pool.tile(
                    [P, N], U8, name="z_scales", tag="z_scales", align_bytes=64
                )

        def interleave_z(g, xh, lo, pool, tag):
            acc = pool.tile([P, PE_COLS_Z, KT], BF16, name="acc_i", tag=tag)
            for b in range(PE_COLS_Z // P):
                cols = slice(lo + b * P, lo + (b + 1) * P)
                nc.tensor.matmul(
                    acc[:, b * P : (b + 1) * P, :],
                    ident_b[:],
                    taps[(g, xh)][:, :, cols].rearrange("f t n -> f n t"),
                    start=True,
                    stop=True,
                )
            return acc

        def copy_interleaved(g, xh, lo, acc, engine_copy):
            engine_copy(
                out=z_grp[(g, xh)][:, lo : lo + PE_COLS_Z, :].rearrange("p n t -> p (n t)").bitcast(F32),
                in_=acc[:].rearrange("p n t -> p (n t)").bitcast(F32),
            )

        def quant_z(g, xh, lo, hi):
            nc.vector.quantize_mx(
                out=z_codes[(g, xh)][:, lo:hi].bitcast(FP8X4),
                scales=z_scales[(g, xh)][:, lo:hi],
                in_=z_grp[(g, xh)][:, lo:hi, :].rearrange("p n t -> p (n t)"),
            )

        def combine(g, nh):
            cols = slice(nh * HALF, (nh + 1) * HALF)
            acc2[(g, nh)] = ps_2.tile([P, HALF], F32, name="acc2", tag="acc2")
            for xh in range(2):
                w = slice(xh * P, (xh + 1) * P)
                nc.tensor.matmul_mx(
                    out=acc2[(g, nh)][:],
                    lhsT=w_codes[:, w].bitcast(FP8X4),
                    lhsT_scale=w_scales[:, w],
                    rhs=z_codes[(g, xh)][:, cols].bitcast(FP8X4),
                    rhs_scale=z_scales[(g, xh)][:, cols],
                    start=(xh == 0),
                    stop=(xh == 1),
                )

        o_sb = {}

        def finish(g, nh):
            if nh == 0:
                o_sb[g] = out_pool.tile([P, N], F32, name="o_sb", tag="o_sb")
            cols = slice(nh * HALF, (nh + 1) * HALF)
            nc.scalar.activation(
                out=o_sb[g][:, cols], in_=acc2[(g, nh)][:], func=RELU, bias=bias[:, 0:1], scale=1.0
            )

        def store(g, lo, hi):
            nc.sync.dma_start(out=out[g][:, lo:hi], in_=o_sb[g][:, lo:hi])

        new_inputs(0)
        load_s_half(0, 0)
        load_s_half(0, 1)
        load_taps(0, KT - 2, KT - 1)
        load_s_half(1, 0)
        load_s_half(1, 1)
        new_inputs(1)
        load_s(1, 0)
        load_s(1, 1)
        load_taps(0, 0, KT - 2)
        load_taps(1, KT - 2, KT - 1)
        load_taps(1, 0, KT - 2)
        ident_f = const.tile([P, P], F32, name="ident_f")
        make_identity(nc, ident_f[:])
        ident_b = const.tile([P, P], BF16, name="ident_b")
        make_identity(nc, ident_b[:])
        b_rows = const.tile([P, P], BF16, name="b_rows")
        nc.vector.memset(b_rows[:], 0.0)
        w_raw = const.tile([P, 2, KT * G], BF16, name="w_raw")
        nc.sync.dma_start(out=w_raw[:, 0, :], in_=weight_A.rearrange("o t f -> o (t f)"))
        nc.sync.dma_start(out=w_raw[:, 1, :], in_=weight_B.rearrange("o t f -> o (t f)"))
        nc.sync.dma_start(out=b_rows[0:1, :], in_=bias_A.rearrange("g o -> o g"))
        nc.sync.dma_start(out=b_rows[1:2, :], in_=bias_B.rearrange("g o -> o g"))
        load_graph(2)

        w_grp = const.tile([P, 2, G, KT], BF16, name="w_grp", align_bytes=64)
        w_codes = const.tile([P, 2 * G], U32, name="w_codes", align_bytes=64)
        w_scales = const.tile([P, 2 * G], U8, name="w_scales", align_bytes=64)
        b_cols = const.tile([P, 2], F32, name="b_cols")
        bias = const.tile([P, 1], F32, name="bias")

        def transpose_weights():
            wt = ps_t.tile([P, 2, KT, G], BF16, name="wt", tag="tp")
            for w in range(2):
                for t in range(KT):
                    nc.tensor.transpose(
                        wt[:, w, t, :], w_raw[:, w, t * G : (t + 1) * G], ident_b[:]
                    )
            nc.scalar.copy(out=w_grp[:], in_=wt[:].rearrange("p w t o -> p w o t"))
            bt = ps_t.tile([P, P], BF16, name="bt", tag="tp")
            nc.tensor.transpose(bt[:], b_rows[:], ident_b[:])
            nc.scalar.copy(out=b_cols[:], in_=bt[:, 0:2])

        def quant_weights():
            nc.vector.quantize_mx(
                out=w_codes[:].bitcast(FP8X4),
                scales=w_scales[:],
                in_=w_grp[:].rearrange("p w o t -> p (w o t)"),
            )
            nc.vector.tensor_add(out=bias[:], in0=b_cols[:, 0:1], in1=b_cols[:, 1:2])

        new_s_grp(0, 0)
        new_s_grp(0, 1)
        regroup_s_half(0, 0)
        regroup_s_half(0, 1)
        transpose_x2(0)
        quant_s(0, 0)
        regroup_s_half(1, 0)
        regroup_s_half(1, 1)
        quant_xt(0)
        quant_s(0, 1)
        for i in range(B - 1):
            shift(i, 0, 0)
            shift(i, 0, 1)
            regroup_s(i + 1, 0)
            if 1 <= i:
                quant_z(i - 1, 0, 0, N)
            regroup_s(i + 1, 1)
            if i == 1:
                quant_weights()
            if 1 <= i:
                quant_z(i - 1, 1, 0, N)
            new_z(i)
            regroup(z_grp[(i, 0)], taps[(i, 0)], V_COLS_Z[i], PE_LO_Z, nc.scalar.copy)
            transpose_x2(i + 1)
            shift(i, 1, 0)
            shift(i, 1, 1)
            acc = interleave_z(i, 0, PE_LO_Z, ps_i, "acc_i")
            quant_s(i + 1, 0)
            regroup(z_grp[(i, 0)], taps[(i, 0)], 0, V_COLS_Z[i], nc.vector.tensor_copy)
            quant_s(i + 1, 1)
            if 1 <= i:
                combine(i - 1, 0)
                combine(i - 1, 1)
            copy_interleaved(i, 0, PE_LO_Z, acc, nc.scalar.copy)
            acc = interleave_z(i, 1, PE_LO_Z, ps_i, "acc_i")
            regroup(z_grp[(i, 1)], taps[(i, 1)], V_COLS_Z[i], PE_LO_Z, nc.scalar.copy)
            regroup(z_grp[(i, 1)], taps[(i, 1)], 0, V_COLS_Z[i], nc.vector.tensor_copy)
            if 1 <= i:
                finish(i - 1, 0)
                finish(i - 1, 1)
                store(i - 1, 0, N)
            if i == 0:
                transpose_weights()
            copy_interleaved(i, 1, PE_LO_Z, acc, nc.scalar.copy)
            quant_xt(i + 1)
            if i + 3 < B:
                load_graph(i + 3)

        g = B - 1
        v_copy = nc.vector.tensor_copy
        s_copy = nc.scalar.copy
        new_z(g)
        halves = [slice(0, HALF), slice(HALF, N)]
        split = [nh * HALF + V_COLS_Z[g] // 2 for nh in range(2)]
        a0 = shift_mm(g, 0, 0, ps_1, "acc1")
        a1 = shift_mm(g, 1, 0, ps_1, "acc1")
        a2 = shift_mm(g, 0, 1, ps_1, "acc1")
        a3 = shift_mm(g, 1, 1, ps_t, "tp")
        quant_z(g - 1, 0, 0, N)
        copy_shift(g, 0, 0, a0, v_copy)
        copy_shift(g, 1, 0, a1, v_copy)
        regroup(z_grp[(g, 0)], taps[(g, 0)], 0, split[0], v_copy)
        quant_z(g - 1, 1, 0, N)
        copy_shift(g, 0, 1, a2, s_copy)
        copy_shift(g, 1, 1, a3, s_copy)
        combine(g - 1, 0)
        combine(g - 1, 1)
        regroup(z_grp[(g, 0)], taps[(g, 0)], split[0], HALF, s_copy)
        regroup(z_grp[(g, 1)], taps[(g, 1)], split[0], HALF, s_copy)
        regroup(z_grp[(g, 1)], taps[(g, 1)], 0, split[0], v_copy)
        finish(g - 1, 0)
        quant_z(g, 0, 0, HALF)
        regroup(z_grp[(g, 0)], taps[(g, 0)], split[1], N, s_copy)
        regroup(z_grp[(g, 0)], taps[(g, 0)], HALF, split[1], v_copy)
        quant_z(g, 1, 0, HALF)
        regroup(z_grp[(g, 1)], taps[(g, 1)], HALF, split[1], v_copy)
        regroup(z_grp[(g, 1)], taps[(g, 1)], split[1], N, s_copy)
        finish(g - 1, 1)
        store(g - 1, 0, N)
        quant_z(g, 0, HALF, N)
        combine(g, 0)
        finish(g, 0)
        store(g, 0, HALF)
        quant_z(g, 1, HALF, N)
        combine(g, 1)
        finish(g, 1)
        store(g, HALF, N)
